import numpy as np
import ml_dtypes


def mxq(x, axis, fmt="e4m3"):
    dtype, down = {"e4m3": (ml_dtypes.float8_e4m3fn, 7), "e5m2": (ml_dtypes.float8_e5m2, 14)}[fmt]
    v = np.moveaxis(np.asarray(x, np.float32).astype(ml_dtypes.bfloat16).astype(np.float64), axis, -1)
    blocks = v.reshape(v.shape[:-1] + (-1, 32))
    amax = np.abs(blocks).max(-1, keepdims=True)
    byte = np.maximum(np.where(amax > 0, np.frexp(amax)[1] - 1 + 127, 0) - down, 1)
    scale = np.exp2(byte - 127.0)
    codes = (blocks / scale).astype(np.float32).astype(dtype).astype(np.float64)
    return np.moveaxis((codes * scale).reshape(v.shape), -1, axis)


WIDE = False


def mx_kscale(k):
    if not WIDE:
        return np.ones(k)
    levels = np.array([10, -10, 5, -5, 0])
    if k % 512:
        return np.exp2(np.random.permutation(np.resize(levels, k // 32))).repeat(32)
    a = np.empty((k // 512, 16))
    for p in range(k // 512):
        a[p, :8] = np.random.permutation(np.resize(levels, 8))
        for g in range(8):
            far = levels[np.abs(levels - a[p, g]) >= 10]
            a[p, g + 8] = far[np.random.randint(len(far))]
    return np.exp2(a.ravel()).repeat(32)


BF16 = ml_dtypes.bfloat16


def bf(x):
    return np.asarray(x, np.float32).astype(BF16)


def f64(x):
    return np.asarray(x).astype(np.float64)


B, C, HH, WW, M, L, G, HID = 2, 1024, 8, 8, 128, 512, 256, 1024
N = HH * WW
ITERS = 3
DUST = 1.0


def lse(a, axis):
    top = a.max(axis=axis, keepdims=True)
    return np.log(np.exp(a - top).sum(axis=axis)) + np.squeeze(top, axis=axis)


def setup_inputs():
    s, t = mx_kscale(C), mx_kscale(HID)
    return {
        "x": bf(np.random.standard_normal((B, C, HH, WW)) * s[None, :, None, None]),
        "Ws1": bf(np.random.standard_normal((HID, C)) / np.sqrt(C) / s[None, :] * t[:, None]),
        "bs1": bf(np.random.standard_normal(HID) * 0.3 * t),
        "Ws2": bf(np.random.standard_normal((M, HID)) * 2.0 / np.sqrt(HID) / t[None, :]),
    }


def reference(x, Ws1, bs1, Ws2):
    xf = f64(x).reshape(B, C, N)
    hs = np.maximum((mxq(f64(Ws1), 1, "e4m3") @ mxq(xf, 1, "e4m3")) + f64(bs1)[None, :, None], 0.0)
    p = mxq(f64(Ws2), 1, "e4m3") @ mxq(hs, 1, "e4m3")
    norm = -np.log(M + N)
    log_mu = np.concatenate([np.full(M, norm), np.full(1, np.log(N) + norm)])
    log_nu = np.full(N, norm)
    Z = np.concatenate([p, np.full((B, 1, N), DUST)], axis=1)
    u = np.zeros((B, M + 1))
    v = np.zeros((B, N))
    for _ in range(ITERS):
        u = log_mu[None] - lse(Z + v[:, None, :], 2)
        v = log_nu[None] - lse(Z + u[:, :, None], 1)
    return np.exp(Z + u[:, :, None] + v[:, None, :] - norm)[:, :-1, :]

@@ -1,0 +1,223 @@
+from contextlib import ExitStack
+
+import concourse.mybir as mybir
+from concourse.masks import make_identity
+
+F32 = mybir.dt.float32
+BF16 = mybir.dt.bfloat16
+U32 = mybir.dt.uint32
+U8 = mybir.dt.uint8
+FP8X4 = mybir.dt.float8_e4m3fn_x4
+ACT = mybir.ActivationFunctionType
+ALU = mybir.AluOpType
+AXIS = mybir.AxisListType
+
+P = 128
+IMAGES = 2
+PIXELS = 64
+COLS = IMAGES * PIXELS
+K = 1024
+PACK = 4
+PASSES = K // (P * PACK)
+HALVES = 2
+ROW_TILES = K // P
+LEAD = 2
+ROUNDS = 3
+
+FLOPS = 2 * K * K * COLS + 2 * P * K * COLS
+
+
+def tile_salad_pa_s_kernel(tc, x, Ws1, bs1, Ws2, out):
+    nc = tc.nc
+    with ExitStack() as stack:
+        stack.enter_context(tc.manual_schedule())
+        keep = stack.enter_context(tc.tile_pool(name="keep", bufs=1))
+        stage = stack.enter_context(tc.tile_pool(name="stage", bufs=4))
+        small = stack.enter_context(tc.tile_pool(name="small", bufs=2))
+        banks = stack.enter_context(tc.psum_pool(name="banks", bufs=5))
+        held_banks = stack.enter_context(tc.psum_pool(name="held", bufs=1))
+
+        w1_rows = keep.tile([P, ROW_TILES, K], BF16)
+        w1_view = Ws1.rearrange("(a p t) c -> a t p c", a=PASSES, t=PACK)
+        x_raw = keep.tile([P, K], BF16)
+        w2_rows = keep.tile([P, K], BF16)
+        for i in range(ROW_TILES):
+            nc.sync.dma_start(out=w1_rows[:, i, :], in_=w1_view[i // PACK, i % PACK])
+            if i == 0:
+                nc.sync.dma_start(
+                    out=x_raw[:].rearrange("q (a f) -> q a f", a=IMAGES * PASSES),
+                    in_=x.rearrange("b (a q t) h w -> q (b a) (t h w)", a=PASSES, t=PACK),
+                )
+        nc.sync.dma_start(out=w2_rows[:], in_=Ws2)
+        bias_bf = keep.tile([P, ROW_TILES], BF16)
+        nc.scalar.dma_start(
+            out=bias_bf[:].rearrange("p (a t) -> p a t", t=PACK),
+            in_=bs1.rearrange("(a p t) -> p a t", a=PASSES, t=PACK),
+        )
+
+        ident = keep.tile([P, P], F32)
+        make_identity(nc, ident[:])
+        mean_of_pixels = keep.tile([P, P], F32)
+        nc.vector.memset(mean_of_pixels[:], 1.0 / PIXELS)
+        col_factor = keep.tile([P, IMAGES], F32)
+        nc.vector.memset(col_factor[:], 0.0)
+        ones = keep.tile([P, IMAGES], F32)
+        nc.vector.memset(ones[:], 1.0)
+        warm = keep.tile([P, 1], F32)
+        nc.vector.memset(warm[:], 0.0)
+        nc.scalar.activation(out=warm[:], in_=warm[:], func=ACT.Exp)
+
+        def flip_and_quantise(rows, codes, scales):
+            words = rows.bitcast(F32).rearrange("r (g w u) -> r g u w", g=PASSES, u=HALVES)
+            flipped = banks.tile([P, PASSES * HALVES * P], F32, tag="bank")
+            for a in range(PASSES * HALVES):
+                nc.tensor.transpose(flipped[:, a * P : (a + 1) * P], words[:, a // HALVES, a % HALVES, :], ident[:])
+            grouped = stage.tile([P, K], BF16, align_bytes=64)
+            nc.scalar.copy(
+                out=grouped[:].bitcast(F32).rearrange("q (g r u) -> q g r u", g=PASSES, u=HALVES),
+                in_=flipped[:].rearrange("q (g u r) -> q g r u", g=PASSES, u=HALVES),
+            )
+            nc.vector.quantize_mx(
+                out=codes.rearrange("q g r -> q (g r)").bitcast(FP8X4),
+                scales=scales.rearrange("q g r -> q (g r)"),
+                in_=grouped[:],
+            )
+
+        x_grouped = keep.tile([P, K], BF16, align_bytes=64)
+        x_codes = keep.tile([P, PASSES, COLS], U32, align_bytes=64)
+        x_scales = keep.tile([P, PASSES, COLS], U8, align_bytes=64)
+        x_from = x_raw[:].rearrange("q (b g t n) -> q g b n t", b=IMAGES, g=PASSES, t=PACK)
+        x_to = x_grouped[:].rearrange("q (g b n t) -> q g b n t", g=PASSES, b=IMAGES, t=PACK)
+        for g in range(PASSES):
+            nc.vector.tensor_copy(out=x_to[:, g], in_=x_from[:, g])
+        nc.vector.quantize_mx(
+            out=x_codes[:].rearrange("q g c -> q (g c)").bitcast(FP8X4),
+            scales=x_scales[:].rearrange("q g c -> q (g c)"),
+            in_=x_grouped[:],
+        )
+        w2_codes = keep.tile([P, PASSES, P], U32, align_bytes=64)
+        w2_scales = keep.tile([P, PASSES, P], U8, align_bytes=64)
+
+        w1_codes = keep.tile([P, ROW_TILES, PASSES, P], U32, align_bytes=64)
+        w1_scales = keep.tile([P, ROW_TILES, PASSES, P], U8, align_bytes=64)
+        hs_codes = keep.tile([P, PASSES, COLS], U32, align_bytes=64)
+        hs_scales = keep.tile([P, PASSES, COLS], U8, align_bytes=64)
+        hidden = [held_banks.tile([P, PACK, COLS], F32, name="hidden%d" % g) for g in range(PASSES)]
+        scores = held_banks.tile([P, COLS], F32)
+
+        def first_product(i):
+            for g in range(PASSES):
+                nc.tensor.matmul_mx(
+                    out=hidden[i // PACK][:, i % PACK, :],
+                    lhsT=w1_codes[:, i, g, :].bitcast(FP8X4),
+                    lhsT_scale=w1_scales[:, i, g, :],
+                    rhs=x_codes[:, g, :].bitcast(FP8X4),
+                    rhs_scale=x_scales[:, g, :],
+                    start=(g == 0),
+                    stop=(g == PASSES - 1),
+                )
+
+        def quantise_hidden(g):
+            summed = stage.tile([P, COLS * PACK], BF16)
+            nc.vector.tensor_tensor(
+                out=summed[:].rearrange("p (c t) -> p c t", t=PACK),
+                in0=hidden[g][:].rearrange("p t c -> p c t"),
+                in1=bias_bf[:, g * PACK : (g + 1) * PACK].unsqueeze(1).to_broadcast([P, COLS, PACK]),
+                op=ALU.add,
+            )
+            hs_grouped = stage.tile([P, COLS * PACK], BF16, align_bytes=64)
+            nc.vector.tensor_scalar_max(out=hs_grouped[:], in0=summed[:], scalar1=0.0)
+            nc.vector.quantize_mx(
+                out=hs_codes[:, g, :].bitcast(FP8X4), scales=hs_scales[:, g, :], in_=hs_grouped[:]
+            )
+
+        def second_product(g):
+            nc.tensor.matmul_mx(
+                out=scores[:],
+                lhsT=w2_codes[:, g, :].bitcast(FP8X4),
+                lhsT_scale=w2_scales[:, g, :],
+                rhs=hs_codes[:, g, :].bitcast(FP8X4),
+                rhs_scale=hs_scales[:, g, :],
+                start=(g == 0),
+                stop=(g == PASSES - 1),
+            )
+
+        to_flip = [(w1_rows[:, i, :], w1_codes[:, i], w1_scales[:, i]) for i in range(ROW_TILES)]
+        to_flip.append((w2_rows[:], w2_codes[:], w2_scales[:]))
+        n_flipped = 0
+        for g in range(PASSES):
+            ahead = min((g + 1) * PACK + LEAD, len(to_flip))
+            for rows, codes, scales in to_flip[n_flipped:ahead]:
+                flip_and_quantise(rows, codes, scales)
+            n_flipped = ahead
+            for t in range(PACK):
+                first_product(g * PACK + t)
+            quantise_hidden(g)
+        for g in range(PASSES):
+            second_product(g)
+
+        col_sums = banks.tile([P, IMAGES], F32, tag="bank")
+        nc.tensor.matmul(out=col_sums[:], lhsT=ident[:], rhs=ones[:], start=True, stop=False)
+        neg_top = small.tile([P, IMAGES], F32)
+        nc.vector.tensor_reduce(
+            out=neg_top[:],
+            in_=scores[:].rearrange("m (b n) -> m b n", b=IMAGES),
+            axis=AXIS.X,
+            op=ALU.max,
+            negate=True,
+        )
+        kern = keep.tile([P, COLS], F32)
+        first_sums = small.tile([P, IMAGES], F32)
+        for b in range(IMAGES):
+            pixels = slice(b * PIXELS, (b + 1) * PIXELS)
+            nc.scalar.activation(
+                out=kern[:, pixels],
+                in_=scores[:, pixels],
+                func=ACT.Exp,
+                bias=neg_top[:, b : b + 1],
+                scale=1.0,
+                accum_out=first_sums[:, b : b + 1],
+            )
+        row_factor = small.tile([P, IMAGES], F32, tag="row_factor")
+        nc.vector.reciprocal(out=row_factor[:], in_=first_sums[:])
+
+        kern_flipped = banks.tile([P, P], F32, tag="bank")
+        nc.tensor.transpose(kern_flipped[:], kern[:], ident[:])
+        kern_t = keep.tile([P, P], F32)
+        nc.scalar.copy(out=kern_t[:], in_=kern_flipped[:])
+
+        last_col_factor = keep.tile([P, 1], F32)
+        for r in range(ROUNDS):
+            nc.tensor.matmul(out=col_sums[:], lhsT=kern[:], rhs=row_factor[:], start=False, stop=True)
+            for b in range(IMAGES):
+                rows = slice(b * PIXELS, (b + 1) * PIXELS)
+                if r == ROUNDS - 1:
+                    nc.vector.reciprocal(out=last_col_factor[rows, :], in_=col_sums[rows, b : b + 1])
+                else:
+                    nc.vector.reciprocal(out=col_factor[rows, b : b + 1], in_=col_sums[rows, b : b + 1])
+            if r == ROUNDS - 1:
+                break
+            dust_sums = banks.tile([P, IMAGES], F32, tag="bank")
+            nc.tensor.matmul(out=dust_sums[:], lhsT=mean_of_pixels[:], rhs=col_factor[:], start=True, stop=True)
+            row_sums = banks.tile([P, IMAGES], F32, tag="bank")
+            nc.tensor.matmul(out=row_sums[:], lhsT=kern_t[:], rhs=col_factor[:], start=True, stop=True)
+            dust_factor = small.tile([P, IMAGES], F32, tag="dust_factor")
+            nc.vector.reciprocal(out=dust_factor[:], in_=dust_sums[:])
+            col_sums = banks.tile([P, IMAGES], F32, tag="bank")
+            nc.tensor.matmul(out=col_sums[:], lhsT=ident[:], rhs=dust_factor[:], start=True, stop=False)
+            row_factor = small.tile([P, IMAGES], F32, tag="row_factor")
+            nc.vector.reciprocal(out=row_factor[:], in_=row_sums[:])
+
+        weighted = keep.tile([P, COLS], F32)
+        for b in range(IMAGES):
+            pixels = slice(b * PIXELS, (b + 1) * PIXELS)
+            nc.scalar.activation(
+                out=weighted[:, pixels], in_=kern[:, pixels], func=ACT.Copy, scale=row_factor[:, b : b + 1]
+            )
+        spread = banks.tile([P, P], F32, tag="bank")
+        nc.tensor.transpose(spread[:], last_col_factor[:, 0:1].to_broadcast([P, P]), ident[:])
+        result = keep.tile([P, COLS], F32)
+        nc.vector.tensor_tensor(out=result[:], in0=weighted[:], in1=spread[:], op=ALU.mult)
+        nc.sync.dma_start(
+            out=out.rearrange("b m n -> m b n"), in_=result[:].rearrange("m (b n) -> m b n", b=IMAGES)
+        )

@@ -23,6 +23,7 @@ HALVES = 2
 ROW_TILES = K // P
 LEAD = 2
 ROUNDS = 3
+FAR = 2.0**100
 
 FLOPS = 2 * K * K * COLS + 2 * P * K * COLS
 
@@ -58,11 +59,13 @@ def tile_salad_pa_s_kernel(tc, x, Ws1, bs1, Ws2, out):
         ident = keep.tile([P, P], F32)
         make_identity(nc, ident[:])
         mean_of_pixels = keep.tile([P, P], F32)
-        nc.vector.memset(mean_of_pixels[:], 1.0 / PIXELS)
-        col_factor = keep.tile([P, IMAGES], F32)
-        nc.vector.memset(col_factor[:], 0.0)
-        ones = keep.tile([P, IMAGES], F32)
-        nc.vector.memset(ones[:], 1.0)
+        nc.vector.memset(mean_of_pixels[:], 0.0)
+        first_dust = keep.tile([P, IMAGES], F32)
+        nc.vector.memset(first_dust[:], FAR)
+        for b in range(IMAGES):
+            own = slice(b * PIXELS, (b + 1) * PIXELS)
+            nc.vector.memset(mean_of_pixels[own, own], 1.0 / PIXELS)
+            nc.vector.memset(first_dust[own, b : b + 1], 1.0)
         warm = keep.tile([P, 1], F32)
         nc.vector.memset(warm[:], 0.0)
         nc.scalar.activation(out=warm[:], in_=warm[:], func=ACT.Exp)
@@ -156,8 +159,6 @@ def tile_salad_pa_s_kernel(tc, x, Ws1, bs1, Ws2, out):
         for g in range(PASSES):
             second_product(g)
 
-        col_sums = banks.tile([P, IMAGES], F32, tag="bank")
-        nc.tensor.matmul(out=col_sums[:], lhsT=ident[:], rhs=ones[:], start=True, stop=False)
         neg_top = small.tile([P, IMAGES], F32)
         nc.vector.tensor_reduce(
             out=neg_top[:],
@@ -186,27 +187,28 @@ def tile_salad_pa_s_kernel(tc, x, Ws1, bs1, Ws2, out):
         kern_t = keep.tile([P, P], F32)
         nc.scalar.copy(out=kern_t[:], in_=kern_flipped[:])
 
+        dust_factor = first_dust
         last_col_factor = keep.tile([P, 1], F32)
         for r in range(ROUNDS):
-            nc.tensor.matmul(out=col_sums[:], lhsT=kern[:], rhs=row_factor[:], start=False, stop=True)
-            for b in range(IMAGES):
-                rows = slice(b * PIXELS, (b + 1) * PIXELS)
-                if r == ROUNDS - 1:
-                    nc.vector.reciprocal(out=last_col_factor[rows, :], in_=col_sums[rows, b : b + 1])
-                else:
-                    nc.vector.reciprocal(out=col_factor[rows, b : b + 1], in_=col_sums[rows, b : b + 1])
+            col_sums = banks.tile([P, IMAGES], F32, tag="bank")
+            nc.tensor.matmul(out=col_sums[:], lhsT=kern[:], rhs=row_factor[:], start=True, stop=True)
+            with_dust = small.tile([P, IMAGES], F32, tag="with_dust")
+            nc.vector.tensor_tensor(out=with_dust[:], in0=col_sums[:], in1=dust_factor[:], op=ALU.add)
             if r == ROUNDS - 1:
+                for b in range(IMAGES):
+                    own = slice(b * PIXELS, (b + 1) * PIXELS)
+                    nc.vector.reciprocal(out=last_col_factor[own, :], in_=with_dust[own, b : b + 1])
                 break
-            dust_sums = banks.tile([P, IMAGES], F32, tag="bank")
-            nc.tensor.matmul(out=dust_sums[:], lhsT=mean_of_pixels[:], rhs=col_factor[:], start=True, stop=True)
+            col_factor = small.tile([P, IMAGES], F32, tag="col_factor")
+            nc.vector.reciprocal(out=col_factor[:], in_=with_dust[:])
             row_sums = banks.tile([P, IMAGES], F32, tag="bank")
             nc.tensor.matmul(out=row_sums[:], lhsT=kern_t[:], rhs=col_factor[:], start=True, stop=True)
-            dust_factor = small.tile([P, IMAGES], F32, tag="dust_factor")
-            nc.vector.reciprocal(out=dust_factor[:], in_=dust_sums[:])
-            col_sums = banks.tile([P, IMAGES], F32, tag="bank")
-            nc.tensor.matmul(out=col_sums[:], lhsT=ident[:], rhs=dust_factor[:], start=True, stop=False)
+            dust_sums = banks.tile([P, IMAGES], F32, tag="bank")
+            nc.tensor.matmul(out=dust_sums[:], lhsT=mean_of_pixels[:], rhs=col_factor[:], start=True, stop=True)
             row_factor = small.tile([P, IMAGES], F32, tag="row_factor")
             nc.vector.reciprocal(out=row_factor[:], in_=row_sums[:])
+            dust_factor = small.tile([P, IMAGES], F32, tag="dust_factor")
+            nc.vector.reciprocal(out=dust_factor[:], in_=dust_sums[:])
 
         weighted = keep.tile([P, COLS], F32)
         for b in range(IMAGES):

@@ -21,7 +21,6 @@ PACK = 4
 PASSES = K // (P * PACK)
 HALVES = 2
 ROW_TILES = K // P
-LEAD = 2
 ROUNDS = 3
 FAR = 2.0**100
 
@@ -35,7 +34,7 @@ def tile_salad_pa_s_kernel(tc, x, Ws1, bs1, Ws2, out):
         keep = stack.enter_context(tc.tile_pool(name="keep", bufs=1))
         stage = stack.enter_context(tc.tile_pool(name="stage", bufs=4))
         small = stack.enter_context(tc.tile_pool(name="small", bufs=2))
-        banks = stack.enter_context(tc.psum_pool(name="banks", bufs=5))
+        banks = stack.enter_context(tc.psum_pool(name="banks", bufs=4))
         held_banks = stack.enter_context(tc.psum_pool(name="held", bufs=1))
 
         w1_rows = keep.tile([P, ROW_TILES, K], BF16)
@@ -44,7 +43,7 @@ def tile_salad_pa_s_kernel(tc, x, Ws1, bs1, Ws2, out):
         w2_rows = keep.tile([P, K], BF16)
         for i in range(ROW_TILES):
             nc.sync.dma_start(out=w1_rows[:, i, :], in_=w1_view[i // PACK, i % PACK])
-            if i == 0:
+            if i == 1:
                 nc.sync.dma_start(
                     out=x_raw[:].rearrange("q (a f) -> q a f", a=IMAGES * PASSES),
                     in_=x.rearrange("b (a q t) h w -> q (b a) (t h w)", a=PASSES, t=PACK),
@@ -70,48 +69,68 @@ def tile_salad_pa_s_kernel(tc, x, Ws1, bs1, Ws2, out):
         nc.vector.memset(warm[:], 0.0)
         nc.scalar.activation(out=warm[:], in_=warm[:], func=ACT.Exp)
 
-        def flip_and_quantise(rows, codes, scales):
-            words = rows.bitcast(F32).rearrange("r (g w u) -> r g u w", g=PASSES, u=HALVES)
-            flipped = banks.tile([P, PASSES * HALVES * P], F32, tag="bank")
-            for a in range(PASSES * HALVES):
-                nc.tensor.transpose(flipped[:, a * P : (a + 1) * P], words[:, a // HALVES, a % HALVES, :], ident[:])
-            grouped = stage.tile([P, K], BF16, align_bytes=64)
-            nc.scalar.copy(
-                out=grouped[:].bitcast(F32).rearrange("q (g r u) -> q g r u", g=PASSES, u=HALVES),
-                in_=flipped[:].rearrange("q (g u r) -> q g r u", g=PASSES, u=HALVES),
-            )
-            nc.vector.quantize_mx(
-                out=codes.rearrange("q g r -> q (g r)").bitcast(FP8X4),
-                scales=scales.rearrange("q g r -> q (g r)"),
-                in_=grouped[:],
-            )
-
         x_grouped = keep.tile([P, K], BF16, align_bytes=64)
         x_codes = keep.tile([P, PASSES, COLS], U32, align_bytes=64)
         x_scales = keep.tile([P, PASSES, COLS], U8, align_bytes=64)
-        x_from = x_raw[:].rearrange("q (b g t n) -> q g b n t", b=IMAGES, g=PASSES, t=PACK)
-        x_to = x_grouped[:].rearrange("q (g b n t) -> q g b n t", g=PASSES, b=IMAGES, t=PACK)
-        for g in range(PASSES):
-            nc.vector.tensor_copy(out=x_to[:, g], in_=x_from[:, g])
-        nc.vector.quantize_mx(
-            out=x_codes[:].rearrange("q g c -> q (g c)").bitcast(FP8X4),
-            scales=x_scales[:].rearrange("q g c -> q (g c)"),
-            in_=x_grouped[:],
-        )
-        w2_codes = keep.tile([P, PASSES, P], U32, align_bytes=64)
-        w2_scales = keep.tile([P, PASSES, P], U8, align_bytes=64)
-
         w1_codes = keep.tile([P, ROW_TILES, PASSES, P], U32, align_bytes=64)
         w1_scales = keep.tile([P, ROW_TILES, PASSES, P], U8, align_bytes=64)
+        w2_codes = keep.tile([P, PASSES, P], U32, align_bytes=64)
+        w2_scales = keep.tile([P, PASSES, P], U8, align_bytes=64)
         hs_codes = keep.tile([P, PASSES, COLS], U32, align_bytes=64)
         hs_scales = keep.tile([P, PASSES, COLS], U8, align_bytes=64)
-        hidden = [held_banks.tile([P, PACK, COLS], F32, name="hidden%d" % g) for g in range(PASSES)]
-        scores = held_banks.tile([P, COLS], F32)
+        rows_of = [w1_rows[:, i, :] for i in range(ROW_TILES)] + [w2_rows[:]]
+        codes_of = [w1_codes[:, i] for i in range(ROW_TILES)] + [w2_codes[:]]
+        scales_of = [w1_scales[:, i] for i in range(ROW_TILES)] + [w2_scales[:]]
+        grouped_of = [keep.tile([P, K], BF16, align_bytes=64, name="grouped%d" % i) for i in range(ROW_TILES + 1)]
+
+        def flip(i, passes):
+            words = rows_of[i].bitcast(F32).rearrange("r (g w u) -> r g u w", g=PASSES, u=HALVES)
+            flipped = banks.tile([P, len(passes), HALVES, P], F32, tag="bank")
+            for j, g in enumerate(passes):
+                for u in range(HALVES):
+                    nc.tensor.transpose(flipped[:, j, u, :], words[:, g, u, :], ident[:])
+            return flipped
+
+        def regroup(i, passes, flipped, copy):
+            words = grouped_of[i][:].bitcast(F32).rearrange("q (g r u) -> q g r u", g=PASSES, u=HALVES)
+            copy(
+                out=words[:, passes[0] : passes[-1] + 1],
+                in_=flipped[:].rearrange("q g u r -> q g r u"),
+            )
+
+        def quantise(i, passes):
+            chosen = slice(passes[0], passes[-1] + 1)
+            nc.vector.quantize_mx(
+                out=codes_of[i][:, chosen, :].rearrange("q g r -> q (g r)").bitcast(FP8X4),
+                scales=scales_of[i][:, chosen, :].rearrange("q g r -> q (g r)"),
+                in_=grouped_of[i][:, passes[0] * PACK * P : (passes[-1] + 1) * PACK * P],
+            )
+
+        def regroup_x():
+            x_from = x_raw[:].rearrange("q (b g t n) -> q g b n t", b=IMAGES, g=PASSES, t=PACK)
+            x_to = x_grouped[:].rearrange("q (g b n t) -> q g b n t", g=PASSES, b=IMAGES, t=PACK)
+            for g in range(PASSES):
+                nc.vector.tensor_copy(out=x_to[:, g], in_=x_from[:, g])
+
+        def quantise_x():
+            nc.vector.quantize_mx(
+                out=x_codes[:].rearrange("q g c -> q (g c)").bitcast(FP8X4),
+                scales=x_scales[:].rearrange("q g c -> q (g c)"),
+                in_=x_grouped[:],
+            )
+
+        hidden0 = held_banks.tile([P, PACK, COLS], F32, tag="h0", name="hidden0")
+        hidden1a = held_banks.tile([P, 2, COLS], F32)
+        hidden1b = held_banks.tile([P, COLS], F32)
+        hidden1c = held_banks.tile([P, COLS], F32)
+        hidden_of = [hidden0[:, t, :] for t in range(PACK)] + [hidden1a[:, 0, :], hidden1a[:, 1, :], hidden1b[:], hidden1c[:]]
+        summed = keep.tile([P, PASSES, COLS * PACK], BF16)
+        hs_grouped = keep.tile([P, PASSES, COLS * PACK], BF16, align_bytes=64)
 
         def first_product(i):
             for g in range(PASSES):
                 nc.tensor.matmul_mx(
-                    out=hidden[i // PACK][:, i % PACK, :],
+                    out=hidden_of[i],
                     lhsT=w1_codes[:, i, g, :].bitcast(FP8X4),
                     lhsT_scale=w1_scales[:, i, g, :],
                     rhs=x_codes[:, g, :].bitcast(FP8X4),
@@ -120,18 +139,33 @@ def tile_salad_pa_s_kernel(tc, x, Ws1, bs1, Ws2, out):
                     stop=(g == PASSES - 1),
                 )
 
-        def quantise_hidden(g):
-            summed = stage.tile([P, COLS * PACK], BF16)
+        def pair(tile, g, t):
+            return tile[:, g, :].rearrange("p (c t) -> p c t", t=PACK)[:, :, t : t + 2]
+
+        def add_bias(g, hidden, t):
             nc.vector.tensor_tensor(
-                out=summed[:].rearrange("p (c t) -> p c t", t=PACK),
-                in0=hidden[g][:].rearrange("p t c -> p c t"),
-                in1=bias_bf[:, g * PACK : (g + 1) * PACK].unsqueeze(1).to_broadcast([P, COLS, PACK]),
+                out=pair(summed, g, t),
+                in0=hidden[:, t : t + 2, :].rearrange("p t c -> p c t"),
+                in1=bias_bf[:, g * PACK + t : g * PACK + t + 2].unsqueeze(1).to_broadcast([P, COLS, 2]),
                 op=ALU.add,
             )
-            hs_grouped = stage.tile([P, COLS * PACK], BF16, align_bytes=64)
-            nc.vector.tensor_scalar_max(out=hs_grouped[:], in0=summed[:], scalar1=0.0)
+
+        def relu(g, t):
+            nc.vector.tensor_scalar_max(out=pair(hs_grouped, g, t), in0=pair(summed, g, t), scalar1=0.0)
+
+        def bias_and_relu_column(i):
+            g, t = i // PACK, i % PACK
+            nc.scalar.activation(
+                out=hs_grouped[:, g, :].rearrange("p (c t) -> p c t", t=PACK)[:, :, t],
+                in_=hidden_of[i],
+                func=ACT.Relu,
+                bias=bias_bf[:, i : i + 1],
+                scale=1.0,
+            )
+
+        def quantise_hidden(g):
             nc.vector.quantize_mx(
-                out=hs_codes[:, g, :].bitcast(FP8X4), scales=hs_scales[:, g, :], in_=hs_grouped[:]
+                out=hs_codes[:, g, :].bitcast(FP8X4), scales=hs_scales[:, g, :], in_=hs_grouped[:, g, :]
             )
 
         def second_product(g):
@@ -145,18 +179,54 @@ def tile_salad_pa_s_kernel(tc, x, Ws1, bs1, Ws2, out):
                 stop=(g == PASSES - 1),
             )
 
-        to_flip = [(w1_rows[:, i, :], w1_codes[:, i], w1_scales[:, i]) for i in range(ROW_TILES)]
-        to_flip.append((w2_rows[:], w2_codes[:], w2_scales[:]))
-        n_flipped = 0
-        for g in range(PASSES):
-            ahead = min((g + 1) * PACK + LEAD, len(to_flip))
-            for rows, codes, scales in to_flip[n_flipped:ahead]:
-                flip_and_quantise(rows, codes, scales)
-            n_flipped = ahead
-            for t in range(PACK):
-                first_product(g * PACK + t)
-            quantise_hidden(g)
-        for g in range(PASSES):
+        both = list(range(PASSES))
+
+        def flip_and_regroup(i):
+            regroup(i, both, flip(i, both), nc.scalar.copy)
+
+        flip_and_regroup(0)
+        flip_and_regroup(1)
+        quantise(0, both)
+        regroup_x()
+        flip_and_regroup(2)
+        quantise(1, both)
+        quantise_x()
+        flip_and_regroup(3)
+        quantise(2, both)
+        flip_and_regroup(4)
+        quantise(3, both)
+        first_product(0)
+        first_product(1)
+        flip_and_regroup(5)
+        add_bias(0, hidden0[:], 0)
+        quantise(4, both)
+        relu(0, 0)
+        flip_and_regroup(6)
+        first_product(2)
+        first_product(3)
+        quantise(5, both)
+        add_bias(0, hidden0[:], 2)
+        halves = [flip(7, [g]) for g in both]
+        flipped2 = flip(8, both)
+        quantise(6, both)
+        for g in both:
+            regroup(7, [g], halves[g], nc.scalar.copy)
+        relu(0, 2)
+        for i in (4, 5, 6):
+            first_product(i)
+        for g in both:
+            quantise(7, [g])
+        add_bias(1, hidden1a[:], 0)
+        quantise_hidden(0)
+        first_product(7)
+        regroup(8, both, flipped2, nc.scalar.copy)
+        bias_and_relu_column(6)
+        bias_and_relu_column(7)
+        relu(1, 0)
+        quantise(8, both)
+        quantise_hidden(1)
+        scores = held_banks.tile([P, COLS], F32, tag="h0")
+        for g in both:
             second_product(g)
 
         neg_top = small.tile([P, IMAGES], F32)

@@ -22,6 +22,8 @@ PASSES = K // (P * PACK)
 HALVES = 2
 ROW_TILES = K // P
 ROUNDS = 3
+IDLE_COLS = 192
+IDLE_MATMULS = 2
 FAR = 2.0**100
 
 FLOPS = 2 * K * K * COLS + 2 * P * K * COLS
@@ -54,6 +56,12 @@ def tile_salad_pa_s_kernel(tc, x, Ws1, bs1, Ws2, out):
             out=bias_bf[:].rearrange("p (a t) -> p a t", t=PACK),
             in_=bs1.rearrange("(a p t) -> p a t", a=PASSES, t=PACK),
         )
+
+        idle = keep.tile([P, IDLE_COLS], F32)
+        nc.vector.memset(idle[:], 0.0)
+        for i in range(IDLE_MATMULS):
+            nowhere = banks.tile([P, IDLE_COLS], F32, tag="bank")
+            nc.tensor.matmul(out=nowhere[:], lhsT=idle[:, 0:P], rhs=idle[:], start=True, stop=True)
 
         ident = keep.tile([P, P], F32)
         make_identity(nc, ident[:])
@@ -163,6 +171,17 @@ def tile_salad_pa_s_kernel(tc, x, Ws1, bs1, Ws2, out):
                 scale=1.0,
             )
 
+        def idle_pass(columns):
+            nc.tensor.matmul_mx(
+                out=spare[:, 0:columns],
+                lhsT=w1_codes[:, 0, 0, :].bitcast(FP8X4),
+                lhsT_scale=w1_scales[:, 0, 0, :],
+                rhs=w1_codes[:, 0 : columns // (PASSES * P)].rearrange("q i g r -> q (i g r)").bitcast(FP8X4),
+                rhs_scale=w1_scales[:, 0 : columns // (PASSES * P)].rearrange("q i g r -> q (i g r)"),
+                start=True,
+                stop=True,
+            )
+
         def quantise_hidden(g):
             nc.vector.quantize_mx(
                 out=hs_codes[:, g, :].bitcast(FP8X4), scales=hs_scales[:, g, :], in_=hs_grouped[:, g, :]
@@ -225,9 +244,13 @@ def tile_salad_pa_s_kernel(tc, x, Ws1, bs1, Ws2, out):
         relu(1, 0)
         quantise(8, both)
         quantise_hidden(1)
+        spare = held_banks.tile([P, 512], F32, tag="hidden1a")
+        idle_pass(512)
+        idle_pass(256)
         scores = held_banks.tile([P, COLS], F32, tag="h0")
         for g in both:
             second_product(g)
+        idle_pass(512)
 
         neg_top = small.tile([P, IMAGES], F32)
         nc.vector.tensor_reduce(
@@ -262,6 +285,7 @@ def tile_salad_pa_s_kernel(tc, x, Ws1, bs1, Ws2, out):
         for r in range(ROUNDS):
             col_sums = banks.tile([P, IMAGES], F32, tag="bank")
             nc.tensor.matmul(out=col_sums[:], lhsT=kern[:], rhs=row_factor[:], start=True, stop=True)
+            idle_pass(512)
             with_dust = small.tile([P, IMAGES], F32, tag="with_dust")
             nc.vector.tensor_tensor(out=with_dust[:], in0=col_sums[:], in1=dust_factor[:], op=ALU.add)
             if r == ROUNDS - 1:
@@ -275,6 +299,7 @@ def tile_salad_pa_s_kernel(tc, x, Ws1, bs1, Ws2, out):
             nc.tensor.matmul(out=row_sums[:], lhsT=kern_t[:], rhs=col_factor[:], start=True, stop=True)
             dust_sums = banks.tile([P, IMAGES], F32, tag="bank")
             nc.tensor.matmul(out=dust_sums[:], lhsT=mean_of_pixels[:], rhs=col_factor[:], start=True, stop=True)
+            idle_pass(256)
             row_factor = small.tile([P, IMAGES], F32, tag="row_factor")
             nc.vector.reciprocal(out=row_factor[:], in_=row_sums[:])
             dust_factor = small.tile([P, IMAGES], F32, tag="dust_factor")

@@ -251,6 +251,7 @@ def tile_salad_pa_s_kernel(tc, x, Ws1, bs1, Ws2, out):
         for g in both:
             second_product(g)
         idle_pass(512)
+        idle_pass(256)
 
         neg_top = small.tile([P, IMAGES], F32)
         nc.vector.tensor_reduce(
@@ -280,30 +281,32 @@ def tile_salad_pa_s_kernel(tc, x, Ws1, bs1, Ws2, out):
         kern_t = keep.tile([P, P], F32)
         nc.scalar.copy(out=kern_t[:], in_=kern_flipped[:])
 
-        dust_factor = first_dust
+        col_sums = banks.tile([P, IMAGES], F32, tag="bank")
+        nc.tensor.matmul(out=col_sums[:], lhsT=ident[:], rhs=first_dust[:], start=True, stop=False)
         last_col_factor = keep.tile([P, 1], F32)
         for r in range(ROUNDS):
-            col_sums = banks.tile([P, IMAGES], F32, tag="bank")
-            nc.tensor.matmul(out=col_sums[:], lhsT=kern[:], rhs=row_factor[:], start=True, stop=True)
+            nc.tensor.matmul(out=col_sums[:], lhsT=kern[:], rhs=row_factor[:], start=(r > 0), stop=(r == 0))
+            if r > 0:
+                nc.tensor.matmul(out=col_sums[:], lhsT=ident[:], rhs=dust_factor[:], start=False, stop=True)
             idle_pass(512)
-            with_dust = small.tile([P, IMAGES], F32, tag="with_dust")
-            nc.vector.tensor_tensor(out=with_dust[:], in0=col_sums[:], in1=dust_factor[:], op=ALU.add)
+            idle_pass(256)
             if r == ROUNDS - 1:
                 for b in range(IMAGES):
                     own = slice(b * PIXELS, (b + 1) * PIXELS)
-                    nc.vector.reciprocal(out=last_col_factor[own, :], in_=with_dust[own, b : b + 1])
+                    nc.vector.reciprocal(out=last_col_factor[own, :], in_=col_sums[own, b : b + 1])
                 break
             col_factor = small.tile([P, IMAGES], F32, tag="col_factor")
-            nc.vector.reciprocal(out=col_factor[:], in_=with_dust[:])
+            nc.vector.reciprocal(out=col_factor[:], in_=col_sums[:])
             row_sums = banks.tile([P, IMAGES], F32, tag="bank")
             nc.tensor.matmul(out=row_sums[:], lhsT=kern_t[:], rhs=col_factor[:], start=True, stop=True)
             dust_sums = banks.tile([P, IMAGES], F32, tag="bank")
             nc.tensor.matmul(out=dust_sums[:], lhsT=mean_of_pixels[:], rhs=col_factor[:], start=True, stop=True)
-            idle_pass(256)
+            idle_pass(512)
             row_factor = small.tile([P, IMAGES], F32, tag="row_factor")
             nc.vector.reciprocal(out=row_factor[:], in_=row_sums[:])
             dust_factor = small.tile([P, IMAGES], F32, tag="dust_factor")
             nc.vector.reciprocal(out=dust_factor[:], in_=dust_sums[:])
+            col_sums = banks.tile([P, IMAGES], F32, tag="bank")
 
         weighted = keep.tile([P, COLS], F32)
         for b in range(IMAGES):

@@ -43,19 +43,23 @@ def tile_salad_pa_s_kernel(tc, x, Ws1, bs1, Ws2, out):
         w1_view = Ws1.rearrange("(a p t) c -> a t p c", a=PASSES, t=PACK)
         x_raw = keep.tile([P, K], BF16)
         w2_rows = keep.tile([P, K], BF16)
+        bias_bf = keep.tile([P, ROW_TILES], BF16)
         for i in range(ROW_TILES):
-            nc.sync.dma_start(out=w1_rows[:, i, :], in_=w1_view[i // PACK, i % PACK])
+            pieces = PASSES if i == 0 else 1
+            for piece in range(pieces):
+                part = slice(piece * (K // pieces), (piece + 1) * (K // pieces))
+                nc.sync.dma_start(out=w1_rows[:, i, part], in_=w1_view[i // PACK, i % PACK][:, part])
             if i == 1:
                 nc.sync.dma_start(
                     out=x_raw[:].rearrange("q (a f) -> q a f", a=IMAGES * PASSES),
                     in_=x.rearrange("b (a q t) h w -> q (b a) (t h w)", a=PASSES, t=PACK),
                 )
+            if i == 2:
+                nc.sync.dma_start(
+                    out=bias_bf[:].rearrange("p (a t) -> p a t", t=PACK),
+                    in_=bs1.rearrange("(a p t) -> p a t", a=PASSES, t=PACK),
+                )
         nc.sync.dma_start(out=w2_rows[:], in_=Ws2)
-        bias_bf = keep.tile([P, ROW_TILES], BF16)
-        nc.scalar.dma_start(
-            out=bias_bf[:].rearrange("p (a t) -> p a t", t=PACK),
-            in_=bs1.rearrange("(a p t) -> p a t", a=PASSES, t=PACK),
-        )
 
         idle = keep.tile([P, IDLE_COLS], F32)
         nc.vector.memset(idle[:], 0.0)
@@ -171,7 +175,7 @@ def tile_salad_pa_s_kernel(tc, x, Ws1, bs1, Ws2, out):
                 scale=1.0,
             )
 
-        def idle_pass(columns):
+        def idle_pass(spare, columns):
             nc.tensor.matmul_mx(
                 out=spare[:, 0:columns],
                 lhsT=w1_codes[:, 0, 0, :].bitcast(FP8X4),
@@ -238,20 +242,21 @@ def tile_salad_pa_s_kernel(tc, x, Ws1, bs1, Ws2, out):
         add_bias(1, hidden1a[:], 0)
         quantise_hidden(0)
         first_product(7)
+        spare = held_banks.tile([P, 512], F32, tag="h0")
+        idle_pass(spare, 512)
+        idle_pass(spare, 512)
         regroup(8, both, flipped2, nc.scalar.copy)
         bias_and_relu_column(6)
         bias_and_relu_column(7)
         relu(1, 0)
         quantise(8, both)
         quantise_hidden(1)
-        spare = held_banks.tile([P, 512], F32, tag="hidden1a")
-        idle_pass(512)
-        idle_pass(256)
         scores = held_banks.tile([P, COLS], F32, tag="h0")
         for g in both:
             second_product(g)
-        idle_pass(512)
-        idle_pass(256)
+        spare = held_banks.tile([P, 512], F32, tag="hidden1a")
+        idle_pass(spare, 512)
+        idle_pass(spare, 512)
 
         neg_top = small.tile([P, IMAGES], F32)
         nc.vector.tensor_reduce(
@@ -288,8 +293,8 @@ def tile_salad_pa_s_kernel(tc, x, Ws1, bs1, Ws2, out):
             nc.tensor.matmul(out=col_sums[:], lhsT=kern[:], rhs=row_factor[:], start=(r > 0), stop=(r == 0))
             if r > 0:
                 nc.tensor.matmul(out=col_sums[:], lhsT=ident[:], rhs=dust_factor[:], start=False, stop=True)
-            idle_pass(512)
-            idle_pass(256)
+            idle_pass(spare, 512)
+            idle_pass(spare, 256)
             if r == ROUNDS - 1:
                 for b in range(IMAGES):
                     own = slice(b * PIXELS, (b + 1) * PIXELS)
@@ -301,7 +306,7 @@ def tile_salad_pa_s_kernel(tc, x, Ws1, bs1, Ws2, out):
             nc.tensor.matmul(out=row_sums[:], lhsT=kern_t[:], rhs=col_factor[:], start=True, stop=True)
             dust_sums = banks.tile([P, IMAGES], F32, tag="bank")
             nc.tensor.matmul(out=dust_sums[:], lhsT=mean_of_pixels[:], rhs=col_factor[:], start=True, stop=True)
-            idle_pass(512)
+            idle_pass(spare, 512)
             row_factor = small.tile([P, IMAGES], F32, tag="row_factor")
             nc.vector.reciprocal(out=row_factor[:], in_=row_sums[:])
             dust_factor = small.tile([P, IMAGES], F32, tag="dust_factor")

@@ -151,19 +151,19 @@ def tile_salad_pa_s_kernel(tc, x, Ws1, bs1, Ws2, out):
                     stop=(g == PASSES - 1),
                 )
 
-        def pair(tile, g, t):
-            return tile[:, g, :].rearrange("p (c t) -> p c t", t=PACK)[:, :, t : t + 2]
+        def some(tile, g, t, n):
+            return tile[:, g, :].rearrange("p (c t) -> p c t", t=PACK)[:, :, t : t + n]
 
-        def add_bias(g, hidden, t):
+        def add_bias(g, hidden, t, n):
             nc.vector.tensor_tensor(
-                out=pair(summed, g, t),
-                in0=hidden[:, t : t + 2, :].rearrange("p t c -> p c t"),
-                in1=bias_bf[:, g * PACK + t : g * PACK + t + 2].unsqueeze(1).to_broadcast([P, COLS, 2]),
+                out=some(summed, g, t, n),
+                in0=hidden[:, t : t + n, :].rearrange("p t c -> p c t"),
+                in1=bias_bf[:, g * PACK + t : g * PACK + t + n].unsqueeze(1).to_broadcast([P, COLS, n]),
                 op=ALU.add,
             )
 
-        def relu(g, t):
-            nc.vector.tensor_scalar_max(out=pair(hs_grouped, g, t), in0=pair(summed, g, t), scalar1=0.0)
+        def relu(g, t, n):
+            nc.vector.tensor_scalar_max(out=some(hs_grouped, g, t, n), in0=some(summed, g, t, n), scalar1=0.0)
 
         def bias_and_relu_column(i):
             g, t = i // PACK, i % PACK
@@ -208,48 +208,44 @@ def tile_salad_pa_s_kernel(tc, x, Ws1, bs1, Ws2, out):
             regroup(i, both, flip(i, both), nc.scalar.copy)
 
         flip_and_regroup(0)
-        flip_and_regroup(1)
-        quantise(0, both)
         regroup_x()
+        quantise(0, both)
+        flip_and_regroup(1)
         flip_and_regroup(2)
         quantise(1, both)
         quantise_x()
         flip_and_regroup(3)
-        quantise(2, both)
         flip_and_regroup(4)
-        quantise(3, both)
-        first_product(0)
-        first_product(1)
+        quantise(2, both)
         flip_and_regroup(5)
-        add_bias(0, hidden0[:], 0)
+        quantise(3, both)
+        for i in range(PACK):
+            first_product(i)
         quantise(4, both)
-        relu(0, 0)
         flip_and_regroup(6)
-        first_product(2)
-        first_product(3)
-        quantise(5, both)
-        add_bias(0, hidden0[:], 2)
         halves = [flip(7, [g]) for g in both]
         flipped2 = flip(8, both)
-        quantise(6, both)
+        add_bias(0, hidden0[:], 0, PACK)
+        quantise(5, both)
+        relu(0, 0, PACK)
         for g in both:
             regroup(7, [g], halves[g], nc.scalar.copy)
-        relu(0, 2)
+        quantise(6, both)
         for i in (4, 5, 6):
             first_product(i)
         for g in both:
             quantise(7, [g])
-        add_bias(1, hidden1a[:], 0)
-        quantise_hidden(0)
         first_product(7)
         spare = held_banks.tile([P, 512], F32, tag="h0")
         idle_pass(spare, 512)
         idle_pass(spare, 512)
+        add_bias(1, hidden1a[:], 0, 2)
         regroup(8, both, flipped2, nc.scalar.copy)
         bias_and_relu_column(6)
         bias_and_relu_column(7)
-        relu(1, 0)
         quantise(8, both)
+        relu(1, 0, 2)
+        quantise_hidden(0)
         quantise_hidden(1)
         scores = held_banks.tile([P, COLS], F32, tag="h0")
         for g in both:
@@ -293,8 +289,9 @@ def tile_salad_pa_s_kernel(tc, x, Ws1, bs1, Ws2, out):
             nc.tensor.matmul(out=col_sums[:], lhsT=kern[:], rhs=row_factor[:], start=(r > 0), stop=(r == 0))
             if r > 0:
                 nc.tensor.matmul(out=col_sums[:], lhsT=ident[:], rhs=dust_factor[:], start=False, stop=True)
-            idle_pass(spare, 512)
-            idle_pass(spare, 256)
+            if r < ROUNDS - 1:
+                idle_pass(spare, 512)
+                idle_pass(spare, 512)
             if r == ROUNDS - 1:
                 for b in range(IMAGES):
                     own = slice(b * PIXELS, (b + 1) * PIXELS)
@@ -306,7 +303,7 @@ def tile_salad_pa_s_kernel(tc, x, Ws1, bs1, Ws2, out):
             nc.tensor.matmul(out=row_sums[:], lhsT=kern_t[:], rhs=col_factor[:], start=True, stop=True)
             dust_sums = banks.tile([P, IMAGES], F32, tag="bank")
             nc.tensor.matmul(out=dust_sums[:], lhsT=mean_of_pixels[:], rhs=col_factor[:], start=True, stop=True)
-            idle_pass(spare, 512)
+            idle_pass(spare, 256)
             row_factor = small.tile([P, IMAGES], F32, tag="row_factor")
             nc.vector.reciprocal(out=row_factor[:], in_=row_sums[:])
             dust_factor = small.tile([P, IMAGES], F32, tag="dust_factor")

@@ -22,8 +22,6 @@ PASSES = K // (P * PACK)
 HALVES = 2
 ROW_TILES = K // P
 ROUNDS = 3
-IDLE_COLS = 192
-IDLE_MATMULS = 2
 FAR = 2.0**100
 
 FLOPS = 2 * K * K * COLS + 2 * P * K * COLS
@@ -60,12 +58,6 @@ def tile_salad_pa_s_kernel(tc, x, Ws1, bs1, Ws2, out):
                     in_=bs1.rearrange("(a p t) -> p a t", a=PASSES, t=PACK),
                 )
         nc.sync.dma_start(out=w2_rows[:], in_=Ws2)
-
-        idle = keep.tile([P, IDLE_COLS], F32)
-        nc.vector.memset(idle[:], 0.0)
-        for i in range(IDLE_MATMULS):
-            nowhere = banks.tile([P, IDLE_COLS], F32, tag="bank")
-            nc.tensor.matmul(out=nowhere[:], lhsT=idle[:, 0:P], rhs=idle[:], start=True, stop=True)
 
         ident = keep.tile([P, P], F32)
         make_identity(nc, ident[:])
@@ -243,9 +235,9 @@ def tile_salad_pa_s_kernel(tc, x, Ws1, bs1, Ws2, out):
         regroup(8, both, flipped2, nc.scalar.copy)
         bias_and_relu_column(6)
         bias_and_relu_column(7)
-        quantise(8, both)
-        relu(1, 0, 2)
         quantise_hidden(0)
+        relu(1, 0, 2)
+        quantise(8, both)
         quantise_hidden(1)
         scores = held_banks.tile([P, COLS], F32, tag="h0")
         for g in both:

@@ -42,6 +42,8 @@ def tile_salad_pa_s_kernel(tc, x, Ws1, bs1, Ws2, out):
         x_raw = keep.tile([P, K], BF16)
         w2_rows = keep.tile([P, K], BF16)
         bias_bf = keep.tile([P, ROW_TILES], BF16)
+        bias_rows = keep.tile([P, K // PASSES], BF16)
+        nc.vector.memset(bias_rows[:], 0.0)
         for i in range(ROW_TILES):
             pieces = PASSES if i == 0 else 1
             for piece in range(pieces):
@@ -52,11 +54,7 @@ def tile_salad_pa_s_kernel(tc, x, Ws1, bs1, Ws2, out):
                     out=x_raw[:].rearrange("q (a f) -> q a f", a=IMAGES * PASSES),
                     in_=x.rearrange("b (a q t) h w -> q (b a) (t h w)", a=PASSES, t=PACK),
                 )
-            if i == 2:
-                nc.sync.dma_start(
-                    out=bias_bf[:].rearrange("p (a t) -> p a t", t=PACK),
-                    in_=bs1.rearrange("(a p t) -> p a t", a=PASSES, t=PACK),
-                )
+                nc.sync.dma_start(out=bias_rows[0:PASSES, :], in_=bs1.rearrange("(a k) -> a k", a=PASSES))
         nc.sync.dma_start(out=w2_rows[:], in_=Ws2)
 
         ident = keep.tile([P, P], F32)
@@ -108,6 +106,19 @@ def tile_salad_pa_s_kernel(tc, x, Ws1, bs1, Ws2, out):
                 out=codes_of[i][:, chosen, :].rearrange("q g r -> q (g r)").bitcast(FP8X4),
                 scales=scales_of[i][:, chosen, :].rearrange("q g r -> q (g r)"),
                 in_=grouped_of[i][:, passes[0] * PACK * P : (passes[-1] + 1) * PACK * P],
+            )
+
+        def flip_bias():
+            words = bias_rows[:].bitcast(F32).rearrange("r (w u) -> r u w", u=HALVES)
+            flipped = banks.tile([P, HALVES, P], F32, tag="bank")
+            for u in range(HALVES):
+                nc.tensor.transpose(flipped[:, u, :], words[:, u, :], ident[:])
+            return flipped
+
+        def regroup_bias(flipped):
+            nc.vector.tensor_copy(
+                out=bias_bf[:].bitcast(F32).rearrange("p (a u) -> p a u", u=HALVES),
+                in_=flipped[:, :, 0:PASSES].rearrange("p u a -> p a u"),
             )
 
         def regroup_x():
@@ -203,6 +214,8 @@ def tile_salad_pa_s_kernel(tc, x, Ws1, bs1, Ws2, out):
         regroup_x()
         quantise(0, both)
         flip_and_regroup(1)
+        flipped_bias = flip_bias()
+        regroup_bias(flipped_bias)
         flip_and_regroup(2)
         quantise(1, both)
         quantise_x()

@@ -21,6 +21,7 @@ PACK = 4
 PASSES = K // (P * PACK)
 HALVES = 2
 ROW_TILES = K // P
+X_BEHIND = 4
 ROUNDS = 3
 FAR = 2.0**100
 
@@ -49,11 +50,12 @@ def tile_salad_pa_s_kernel(tc, x, Ws1, bs1, Ws2, out):
             for piece in range(pieces):
                 part = slice(piece * (K // pieces), (piece + 1) * (K // pieces))
                 nc.sync.dma_start(out=w1_rows[:, i, part], in_=w1_view[i // PACK, i % PACK][:, part])
-            if i == 1:
+            if i == X_BEHIND:
                 nc.sync.dma_start(
                     out=x_raw[:].rearrange("q (a f) -> q a f", a=IMAGES * PASSES),
                     in_=x.rearrange("b (a q t) h w -> q (b a) (t h w)", a=PASSES, t=PACK),
                 )
+            if i == 1:
                 nc.sync.dma_start(out=bias_rows[0:PASSES, :], in_=bs1.rearrange("(a k) -> a k", a=PASSES))
         nc.sync.dma_start(out=w2_rows[:], in_=Ws2)
 
@@ -128,17 +130,14 @@ def tile_salad_pa_s_kernel(tc, x, Ws1, bs1, Ws2, out):
                 nc.vector.tensor_copy(out=x_to[:, g], in_=x_from[:, g])
 
         def quantise_x():
-            nc.vector.quantize_mx(
-                out=x_codes[:].rearrange("q g c -> q (g c)").bitcast(FP8X4),
-                scales=x_scales[:].rearrange("q g c -> q (g c)"),
-                in_=x_grouped[:],
-            )
+            for g in range(PASSES):
+                nc.vector.quantize_mx(
+                    out=x_codes[:, g, :].bitcast(FP8X4),
+                    scales=x_scales[:, g, :],
+                    in_=x_grouped[:, g * PACK * COLS : (g + 1) * PACK * COLS],
+                )
 
-        hidden0 = held_banks.tile([P, PACK, COLS], F32, tag="h0", name="hidden0")
-        hidden1a = held_banks.tile([P, 2, COLS], F32)
-        hidden1b = held_banks.tile([P, COLS], F32)
-        hidden1c = held_banks.tile([P, COLS], F32)
-        hidden_of = [hidden0[:, t, :] for t in range(PACK)] + [hidden1a[:, 0, :], hidden1a[:, 1, :], hidden1b[:], hidden1c[:]]
+        early_spare = held_banks.tile([P, 512], F32, tag="h0", name="early_spare")
         summed = keep.tile([P, PASSES, COLS * PACK], BF16)
         hs_grouped = keep.tile([P, PASSES, COLS * PACK], BF16, align_bytes=64)
 
@@ -211,31 +210,38 @@ def tile_salad_pa_s_kernel(tc, x, Ws1, bs1, Ws2, out):
             regroup(i, both, flip(i, both), nc.scalar.copy)
 
         flip_and_regroup(0)
-        regroup_x()
-        quantise(0, both)
         flip_and_regroup(1)
         flipped_bias = flip_bias()
+        quantise(0, both)
         regroup_bias(flipped_bias)
         flip_and_regroup(2)
         quantise(1, both)
-        quantise_x()
         flip_and_regroup(3)
-        flip_and_regroup(4)
         quantise(2, both)
-        flip_and_regroup(5)
+        regroup_x()
+        flip_and_regroup(4)
         quantise(3, both)
-        for i in range(PACK):
-            first_product(i)
+        idle_pass(early_spare, 512)
+        idle_pass(early_spare, 256)
+        hidden0 = held_banks.tile([P, PACK, COLS], F32, tag="h0", name="hidden0")
+        hidden1a = held_banks.tile([P, 2, COLS], F32)
+        hidden1b = held_banks.tile([P, COLS], F32)
+        hidden1c = held_banks.tile([P, COLS], F32)
+        hidden_of = [hidden0[:, t, :] for t in range(PACK)] + [hidden1a[:, 0, :], hidden1a[:, 1, :], hidden1b[:], hidden1c[:]]
+        flip_and_regroup(5)
+        quantise_x()
         quantise(4, both)
         flip_and_regroup(6)
+        quantise(5, both)
+        for i in range(PACK):
+            first_product(i)
         halves = [flip(7, [g]) for g in both]
         flipped2 = flip(8, both)
         add_bias(0, hidden0[:], 0, PACK)
-        quantise(5, both)
+        quantise(6, both)
         relu(0, 0, PACK)
         for g in both:
             regroup(7, [g], halves[g], nc.scalar.copy)
-        quantise(6, both)
         for i in (4, 5, 6):
             first_product(i)
         for g in both:
@@ -259,6 +265,8 @@ def tile_salad_pa_s_kernel(tc, x, Ws1, bs1, Ws2, out):
         idle_pass(spare, 512)
         idle_pass(spare, 512)
 
+        col_sums = banks.tile([P, IMAGES], F32, tag="bank")
+        nc.tensor.matmul(out=col_sums[:], lhsT=ident[:], rhs=first_dust[:], start=True, stop=False)
         neg_top = small.tile([P, IMAGES], F32)
         nc.vector.tensor_reduce(
             out=neg_top[:],
@@ -287,8 +295,6 @@ def tile_salad_pa_s_kernel(tc, x, Ws1, bs1, Ws2, out):
         kern_t = keep.tile([P, P], F32)
         nc.scalar.copy(out=kern_t[:], in_=kern_flipped[:])
 
-        col_sums = banks.tile([P, IMAGES], F32, tag="bank")
-        nc.tensor.matmul(out=col_sums[:], lhsT=ident[:], rhs=first_dust[:], start=True, stop=False)
         last_col_factor = keep.tile([P, 1], F32)
         for r in range(ROUNDS):
             nc.tensor.matmul(out=col_sums[:], lhsT=kern[:], rhs=row_factor[:], start=(r > 0), stop=(r == 0))

@@ -137,8 +137,9 @@ def tile_salad_pa_s_kernel(tc, x, Ws1, bs1, Ws2, out):
                     in_=x_grouped[:, g * PACK * COLS : (g + 1) * PACK * COLS],
                 )
 
-        early_spare = held_banks.tile([P, 512], F32, tag="h0", name="early_spare")
+        early_spare = held_banks.tile([P, 512], F32, tag="bank_b", name="early_spare")
         summed = keep.tile([P, PASSES, COLS * PACK], BF16)
+        planes = keep.tile([P, PACK, COLS], BF16)
         hs_grouped = keep.tile([P, PASSES, COLS * PACK], BF16, align_bytes=64)
 
         def first_product(i):
@@ -175,6 +176,17 @@ def tile_salad_pa_s_kernel(tc, x, Ws1, bs1, Ws2, out):
                 func=ACT.Relu,
                 bias=bias_bf[:, i : i + 1],
                 scale=1.0,
+            )
+
+        def bias_and_relu_plane(t):
+            nc.scalar.activation(
+                out=planes[:, t, :], in_=hidden_of[t], func=ACT.Relu, bias=bias_bf[:, t : t + 1], scale=1.0
+            )
+
+        def interleave():
+            nc.vector.tensor_copy(
+                out=hs_grouped[:, 0, :].rearrange("p (c t) -> p c t", t=PACK),
+                in_=planes[:].rearrange("p t c -> p c t"),
             )
 
         def idle_pass(spare, columns):
@@ -223,11 +235,15 @@ def tile_salad_pa_s_kernel(tc, x, Ws1, bs1, Ws2, out):
         quantise(3, both)
         idle_pass(early_spare, 512)
         idle_pass(early_spare, 256)
-        hidden0 = held_banks.tile([P, PACK, COLS], F32, tag="h0", name="hidden0")
-        hidden1a = held_banks.tile([P, 2, COLS], F32)
-        hidden1b = held_banks.tile([P, COLS], F32)
-        hidden1c = held_banks.tile([P, COLS], F32)
-        hidden_of = [hidden0[:, t, :] for t in range(PACK)] + [hidden1a[:, 0, :], hidden1a[:, 1, :], hidden1b[:], hidden1c[:]]
+        hidden_of = {}
+        first_pair = held_banks.tile([P, 2, COLS], F32, tag="bank_a", name="first_pair")
+        second_pair = held_banks.tile([P, 2, COLS], F32, tag="bank_b", name="second_pair")
+        third_pair = held_banks.tile([P, 2, COLS], F32, tag="bank_c", name="third_pair")
+        for j in range(2):
+            hidden_of[j] = first_pair[:, j, :]
+            hidden_of[j + 2] = second_pair[:, j, :]
+            hidden_of[j + 4] = third_pair[:, j, :]
+        hidden_of[7] = held_banks.tile([P, COLS], F32, tag="bank_d", name="hidden7")[:]
         flip_and_regroup(5)
         quantise_x()
         quantise(4, both)
@@ -237,20 +253,22 @@ def tile_salad_pa_s_kernel(tc, x, Ws1, bs1, Ws2, out):
             first_product(i)
         halves = [flip(7, [g]) for g in both]
         flipped2 = flip(8, both)
-        add_bias(0, hidden0[:], 0, PACK)
+        for t in (1, 0, 3, 2):
+            bias_and_relu_plane(t)
         quantise(6, both)
-        relu(0, 0, PACK)
+        interleave()
         for g in both:
             regroup(7, [g], halves[g], nc.scalar.copy)
+        hidden_of[6] = held_banks.tile([P, COLS], F32, tag="bank_a", name="hidden6")[:]
         for i in (4, 5, 6):
             first_product(i)
         for g in both:
             quantise(7, [g])
         first_product(7)
-        spare = held_banks.tile([P, 512], F32, tag="h0")
+        spare = held_banks.tile([P, 512], F32, tag="bank_b")
         idle_pass(spare, 512)
         idle_pass(spare, 512)
-        add_bias(1, hidden1a[:], 0, 2)
+        add_bias(1, third_pair[:], 0, 2)
         regroup(8, both, flipped2, nc.scalar.copy)
         bias_and_relu_column(6)
         bias_and_relu_column(7)
@@ -258,10 +276,10 @@ def tile_salad_pa_s_kernel(tc, x, Ws1, bs1, Ws2, out):
         relu(1, 0, 2)
         quantise(8, both)
         quantise_hidden(1)
-        scores = held_banks.tile([P, COLS], F32, tag="h0")
+        scores = held_banks.tile([P, COLS], F32, tag="bank_b")
         for g in both:
             second_product(g)
-        spare = held_banks.tile([P, 512], F32, tag="hidden1a")
+        spare = held_banks.tile([P, 512], F32, tag="bank_c")
         idle_pass(spare, 512)
         idle_pass(spare, 512)
 

from contextlib import ExitStack

import concourse.mybir as mybir
from concourse.masks import make_identity

F32 = mybir.dt.float32
BF16 = mybir.dt.bfloat16
U32 = mybir.dt.uint32
U8 = mybir.dt.uint8
FP8X4 = mybir.dt.float8_e4m3fn_x4
ACT = mybir.ActivationFunctionType
ALU = mybir.AluOpType
AXIS = mybir.AxisListType

P = 128
IMAGES = 2
PIXELS = 64
COLS = IMAGES * PIXELS
K = 1024
PACK = 4
PASSES = K // (P * PACK)
HALVES = 2
ROW_TILES = K // P
X_BEHIND = 4
ROUNDS = 3
FAR = 2.0**100

FLOPS = 2 * K * K * COLS + 2 * P * K * COLS


def tile_salad_pa_s_kernel(tc, x, Ws1, bs1, Ws2, out):
    nc = tc.nc
    with ExitStack() as stack:
        stack.enter_context(tc.manual_schedule())
        keep = stack.enter_context(tc.tile_pool(name="keep", bufs=1))
        stage = stack.enter_context(tc.tile_pool(name="stage", bufs=4))
        small = stack.enter_context(tc.tile_pool(name="small", bufs=2))
        banks = stack.enter_context(tc.psum_pool(name="banks", bufs=4))
        held_banks = stack.enter_context(tc.psum_pool(name="held", bufs=1))

        w1_rows = keep.tile([P, ROW_TILES, K], BF16)
        w1_view = Ws1.rearrange("(a p t) c -> a t p c", a=PASSES, t=PACK)
        x_raw = keep.tile([P, K], BF16)
        w2_rows = keep.tile([P, K], BF16)
        bias_bf = keep.tile([P, ROW_TILES], BF16)
        bias_rows = keep.tile([P, K // PASSES], BF16)
        nc.vector.memset(bias_rows[:], 0.0)
        for i in range(ROW_TILES):
            pieces = PASSES if i == 0 else 1
            for piece in range(pieces):
                part = slice(piece * (K // pieces), (piece + 1) * (K // pieces))
                nc.sync.dma_start(out=w1_rows[:, i, part], in_=w1_view[i // PACK, i % PACK][:, part])
            if i == X_BEHIND:
                nc.sync.dma_start(
                    out=x_raw[:].rearrange("q (a f) -> q a f", a=IMAGES * PASSES),
                    in_=x.rearrange("b (a q t) h w -> q (b a) (t h w)", a=PASSES, t=PACK),
                )
            if i == 1:
                nc.sync.dma_start(out=bias_rows[0:PASSES, :], in_=bs1.rearrange("(a k) -> a k", a=PASSES))
        nc.sync.dma_start(out=w2_rows[:], in_=Ws2)

        ident = keep.tile([P, P], F32)
        make_identity(nc, ident[:])
        mean_of_pixels = keep.tile([P, P], F32)
        nc.vector.memset(mean_of_pixels[:], 0.0)
        first_dust = keep.tile([P, IMAGES], F32)
        nc.vector.memset(first_dust[:], FAR)
        for b in range(IMAGES):
            own = slice(b * PIXELS, (b + 1) * PIXELS)
            nc.vector.memset(mean_of_pixels[own, own], 1.0 / PIXELS)
            nc.vector.memset(first_dust[own, b : b + 1], 1.0)
        warm = keep.tile([P, 1], F32)
        nc.vector.memset(warm[:], 0.0)
        nc.scalar.activation(out=warm[:], in_=warm[:], func=ACT.Exp)

        x_grouped = keep.tile([P, K], BF16, align_bytes=64)
        x_codes = keep.tile([P, PASSES, COLS], U32, align_bytes=64)
        x_scales = keep.tile([P, PASSES, COLS], U8, align_bytes=64)
        w1_codes = keep.tile([P, ROW_TILES, PASSES, P], U32, align_bytes=64)
        w1_scales = keep.tile([P, ROW_TILES, PASSES, P], U8, align_bytes=64)
        w2_codes = keep.tile([P, PASSES, P], U32, align_bytes=64)
        w2_scales = keep.tile([P, PASSES, P], U8, align_bytes=64)
        hs_codes = keep.tile([P, PASSES, COLS], U32, align_bytes=64)
        hs_scales = keep.tile([P, PASSES, COLS], U8, align_bytes=64)
        rows_of = [w1_rows[:, i, :] for i in range(ROW_TILES)] + [w2_rows[:]]
        codes_of = [w1_codes[:, i] for i in range(ROW_TILES)] + [w2_codes[:]]
        scales_of = [w1_scales[:, i] for i in range(ROW_TILES)] + [w2_scales[:]]
        grouped_of = [keep.tile([P, K], BF16, align_bytes=64, name="grouped%d" % i) for i in range(ROW_TILES + 1)]

        def flip(i, passes):
            words = rows_of[i].bitcast(F32).rearrange("r (g w u) -> r g u w", g=PASSES, u=HALVES)
            flipped = banks.tile([P, len(passes), HALVES, P], F32, tag="bank")
            for j, g in enumerate(passes):
                for u in range(HALVES):
                    nc.tensor.transpose(flipped[:, j, u, :], words[:, g, u, :], ident[:])
            return flipped

        def regroup(i, passes, flipped, copy):
            words = grouped_of[i][:].bitcast(F32).rearrange("q (g r u) -> q g r u", g=PASSES, u=HALVES)
            copy(
                out=words[:, passes[0] : passes[-1] + 1],
                in_=flipped[:].rearrange("q g u r -> q g r u"),
            )

        def quantise(i, passes):
            chosen = slice(passes[0], passes[-1] + 1)
            nc.vector.quantize_mx(
                out=codes_of[i][:, chosen, :].rearrange("q g r -> q (g r)").bitcast(FP8X4),
                scales=scales_of[i][:, chosen, :].rearrange("q g r -> q (g r)"),
                in_=grouped_of[i][:, passes[0] * PACK * P : (passes[-1] + 1) * PACK * P],
            )

        def flip_bias():
            words = bias_rows[:].bitcast(F32).rearrange("r (w u) -> r u w", u=HALVES)
            flipped = banks.tile([P, HALVES, P], F32, tag="bank")
            for u in range(HALVES):
                nc.tensor.transpose(flipped[:, u, :], words[:, u, :], ident[:])
            return flipped

        def regroup_bias(flipped):
            nc.vector.tensor_copy(
                out=bias_bf[:].bitcast(F32).rearrange("p (a u) -> p a u", u=HALVES),
                in_=flipped[:, :, 0:PASSES].rearrange("p u a -> p a u"),
            )

        def regroup_x():
            x_from = x_raw[:].rearrange("q (b g t n) -> q g b n t", b=IMAGES, g=PASSES, t=PACK)
            x_to = x_grouped[:].rearrange("q (g b n t) -> q g b n t", g=PASSES, b=IMAGES, t=PACK)
            for g in range(PASSES):
                nc.vector.tensor_copy(out=x_to[:, g], in_=x_from[:, g])

        def quantise_x():
            for g in range(PASSES):
                nc.vector.quantize_mx(
                    out=x_codes[:, g, :].bitcast(FP8X4),
                    scales=x_scales[:, g, :],
                    in_=x_grouped[:, g * PACK * COLS : (g + 1) * PACK * COLS],
                )

        early_spare = held_banks.tile([P, 512], F32, tag="bank_b", name="early_spare")
        summed = keep.tile([P, PASSES, COLS * PACK], BF16)
        planes = keep.tile([P, PACK, COLS], BF16)
        hs_grouped = keep.tile([P, PASSES, COLS * PACK], BF16, align_bytes=64)

        def first_product(i):
            for g in range(PASSES):
                nc.tensor.matmul_mx(
                    out=hidden_of[i],
                    lhsT=w1_codes[:, i, g, :].bitcast(FP8X4),
                    lhsT_scale=w1_scales[:, i, g, :],
                    rhs=x_codes[:, g, :].bitcast(FP8X4),
                    rhs_scale=x_scales[:, g, :],
                    start=(g == 0),
                    stop=(g == PASSES - 1),
                )

        def some(tile, g, t, n):
            return tile[:, g, :].rearrange("p (c t) -> p c t", t=PACK)[:, :, t : t + n]

        def add_bias(g, hidden, t, n):
            nc.vector.tensor_tensor(
                out=some(summed, g, t, n),
                in0=hidden[:, t : t + n, :].rearrange("p t c -> p c t"),
                in1=bias_bf[:, g * PACK + t : g * PACK + t + n].unsqueeze(1).to_broadcast([P, COLS, n]),
                op=ALU.add,
            )

        def relu(g, t, n):
            nc.vector.tensor_scalar_max(out=some(hs_grouped, g, t, n), in0=some(summed, g, t, n), scalar1=0.0)

        def bias_and_relu_column(i):
            g, t = i // PACK, i % PACK
            nc.scalar.activation(
                out=hs_grouped[:, g, :].rearrange("p (c t) -> p c t", t=PACK)[:, :, t],
                in_=hidden_of[i],
                func=ACT.Relu,
                bias=bias_bf[:, i : i + 1],
                scale=1.0,
            )

        def bias_and_relu_plane(t):
            nc.scalar.activation(
                out=planes[:, t, :], in_=hidden_of[t], func=ACT.Relu, bias=bias_bf[:, t : t + 1], scale=1.0
            )

        def interleave():
            nc.vector.tensor_copy(
                out=hs_grouped[:, 0, :].rearrange("p (c t) -> p c t", t=PACK),
                in_=planes[:].rearrange("p t c -> p c t"),
            )

        def idle_pass(spare, columns):
            nc.tensor.matmul_mx(
                out=spare[:, 0:columns],
                lhsT=w1_codes[:, 0, 0, :].bitcast(FP8X4),
                lhsT_scale=w1_scales[:, 0, 0, :],
                rhs=w1_codes[:, 0 : columns // (PASSES * P)].rearrange("q i g r -> q (i g r)").bitcast(FP8X4),
                rhs_scale=w1_scales[:, 0 : columns // (PASSES * P)].rearrange("q i g r -> q (i g r)"),
                start=True,
                stop=True,
            )

        def quantise_hidden(g):
            nc.vector.quantize_mx(
                out=hs_codes[:, g, :].bitcast(FP8X4), scales=hs_scales[:, g, :], in_=hs_grouped[:, g, :]
            )

        def second_product(g):
            nc.tensor.matmul_mx(
                out=scores[:],
                lhsT=w2_codes[:, g, :].bitcast(FP8X4),
                lhsT_scale=w2_scales[:, g, :],
                rhs=hs_codes[:, g, :].bitcast(FP8X4),
                rhs_scale=hs_scales[:, g, :],
                start=(g == 0),
                stop=(g == PASSES - 1),
            )

        both = list(range(PASSES))

        def flip_and_regroup(i):
            regroup(i, both, flip(i, both), nc.scalar.copy)

        flip_and_regroup(0)
        flip_and_regroup(1)
        flipped_bias = flip_bias()
        quantise(0, both)
        regroup_bias(flipped_bias)
        flip_and_regroup(2)
        quantise(1, both)
        flip_and_regroup(3)
        quantise(2, both)
        regroup_x()
        flip_and_regroup(4)
        quantise(3, both)
        idle_pass(early_spare, 512)
        idle_pass(early_spare, 256)
        hidden_of = {}
        first_pair = held_banks.tile([P, 2, COLS], F32, tag="bank_a", name="first_pair")
        second_pair = held_banks.tile([P, 2, COLS], F32, tag="bank_b", name="second_pair")
        third_pair = held_banks.tile([P, 2, COLS], F32, tag="bank_c", name="third_pair")
        for j in range(2):
            hidden_of[j] = first_pair[:, j, :]
            hidden_of[j + 2] = second_pair[:, j, :]
            hidden_of[j + 4] = third_pair[:, j, :]
        hidden_of[7] = held_banks.tile([P, COLS], F32, tag="bank_d", name="hidden7")[:]
        flip_and_regroup(5)
        quantise_x()
        quantise(4, both)
        flip_and_regroup(6)
        quantise(5, both)
        for i in range(PACK):
            first_product(i)
        halves = [flip(7, [g]) for g in both]
        flipped2 = flip(8, both)
        for t in (1, 0, 3, 2):
            bias_and_relu_plane(t)
        quantise(6, both)
        interleave()
        for g in both:
            regroup(7, [g], halves[g], nc.scalar.copy)
        hidden_of[6] = held_banks.tile([P, COLS], F32, tag="bank_a", name="hidden6")[:]
        for i in (4, 5, 6):
            first_product(i)
        for g in both:
            quantise(7, [g])
        first_product(7)
        spare = held_banks.tile([P, 512], F32, tag="bank_b")
        idle_pass(spare, 512)
        idle_pass(spare, 512)
        add_bias(1, third_pair[:], 0, 2)
        regroup(8, both, flipped2, nc.scalar.copy)
        bias_and_relu_column(6)
        bias_and_relu_column(7)
        quantise_hidden(0)
        relu(1, 0, 2)
        quantise(8, both)
        quantise_hidden(1)
        scores = held_banks.tile([P, COLS], F32, tag="bank_b")
        for g in both:
            second_product(g)
        spare = held_banks.tile([P, 512], F32, tag="bank_c")
        idle_pass(spare, 512)
        idle_pass(spare, 512)

        col_sums = banks.tile([P, IMAGES], F32, tag="bank")
        nc.tensor.matmul(out=col_sums[:], lhsT=ident[:], rhs=first_dust[:], start=True, stop=False)
        neg_top = small.tile([P, IMAGES], F32)
        nc.vector.tensor_reduce(
            out=neg_top[:],
            in_=scores[:].rearrange("m (b n) -> m b n", b=IMAGES),
            axis=AXIS.X,
            op=ALU.max,
            negate=True,
        )
        kern = keep.tile([P, COLS], F32)
        first_sums = small.tile([P, IMAGES], F32)
        for b in range(IMAGES):
            pixels = slice(b * PIXELS, (b + 1) * PIXELS)
            nc.scalar.activation(
                out=kern[:, pixels],
                in_=scores[:, pixels],
                func=ACT.Exp,
                bias=neg_top[:, b : b + 1],
                scale=1.0,
                accum_out=first_sums[:, b : b + 1],
            )
        row_factor = small.tile([P, IMAGES], F32, tag="row_factor")
        nc.vector.reciprocal(out=row_factor[:], in_=first_sums[:])

        kern_flipped = banks.tile([P, P], F32, tag="bank")
        nc.tensor.transpose(kern_flipped[:], kern[:], ident[:])
        kern_t = keep.tile([P, P], F32)
        nc.scalar.copy(out=kern_t[:], in_=kern_flipped[:])

        last_col_factor = keep.tile([P, 1], F32)
        for r in range(ROUNDS):
            nc.tensor.matmul(out=col_sums[:], lhsT=kern[:], rhs=row_factor[:], start=(r > 0), stop=(r == 0))
            if r > 0:
                nc.tensor.matmul(out=col_sums[:], lhsT=ident[:], rhs=dust_factor[:], start=False, stop=True)
            if r < ROUNDS - 1:
                idle_pass(spare, 512)
                idle_pass(spare, 512)
            if r == ROUNDS - 1:
                for b in range(IMAGES):
                    own = slice(b * PIXELS, (b + 1) * PIXELS)
                    nc.vector.reciprocal(out=last_col_factor[own, :], in_=col_sums[own, b : b + 1])
                break
            col_factor = small.tile([P, IMAGES], F32, tag="col_factor")
            nc.vector.reciprocal(out=col_factor[:], in_=col_sums[:])
            row_sums = banks.tile([P, IMAGES], F32, tag="bank")
            nc.tensor.matmul(out=row_sums[:], lhsT=kern_t[:], rhs=col_factor[:], start=True, stop=True)
            dust_sums = banks.tile([P, IMAGES], F32, tag="bank")
            nc.tensor.matmul(out=dust_sums[:], lhsT=mean_of_pixels[:], rhs=col_factor[:], start=True, stop=True)
            idle_pass(spare, 256)
            row_factor = small.tile([P, IMAGES], F32, tag="row_factor")
            nc.vector.reciprocal(out=row_factor[:], in_=row_sums[:])
            dust_factor = small.tile([P, IMAGES], F32, tag="dust_factor")
            nc.vector.reciprocal(out=dust_factor[:], in_=dust_sums[:])
            col_sums = banks.tile([P, IMAGES], F32, tag="bank")

        weighted = keep.tile([P, COLS], F32)
        for b in range(IMAGES):
            pixels = slice(b * PIXELS, (b + 1) * PIXELS)
            nc.scalar.activation(
                out=weighted[:, pixels], in_=kern[:, pixels], func=ACT.Copy, scale=row_factor[:, b : b + 1]
            )
        spread = banks.tile([P, P], F32, tag="bank")
        nc.tensor.transpose(spread[:], last_col_factor[:, 0:1].to_broadcast([P, P]), ident[:])
        result = keep.tile([P, COLS], F32)
        nc.vector.tensor_tensor(out=result[:], in0=weighted[:], in1=spread[:], op=ALU.mult)
        nc.sync.dma_start(
            out=out.rearrange("b m n -> m b n"), in_=result[:].rearrange("m (b n) -> m b n", b=IMAGES)
        )
